import numpy as np
import ml_dtypes

BF16 = ml_dtypes.bfloat16


def bf(x):
    return np.asarray(x, np.float32).astype(BF16)


def f32(x):
    return np.asarray(x, np.float32)


def f64(x):
    return np.asarray(x).astype(np.float64)


def striped(idx):
    return np.tile(idx.reshape(-1, 16).T, (8, 1))


S, D, M, K, R, N = 4096, 128, 256, 16, 128, 2048


def elu(v):
    return np.maximum(v, 0.0) + np.exp(np.minimum(v, 0.0)) - 1.0


def setup_inputs():
    return {"table": bf(np.random.standard_normal((D, S))), "w": bf(3.0 * np.random.standard_normal((D, M)) / np.sqrt(D)), "ew": f32(np.random.uniform(0.0, 1.0, (1, N))), "offs": striped(np.random.permutation(np.tile(np.arange(S), 2))[:N])}


def reference(table, w, ew, offs):
    idx = offs[:16].T.reshape(-1)
    y = f64(w).T @ f64(table)[:, idx]
    z = (y * f64(ew)).reshape(M, R, K).mean(axis=2)
    return elu(z)

@@ -1,0 +1,66 @@
+import concourse.mybir as mybir
+
+BF16 = mybir.dt.bfloat16
+F32 = mybir.dt.float32
+U16 = mybir.dt.uint16
+ALU = mybir.AluOpType
+ACT = mybir.ActivationFunctionType
+
+P = 128
+NODES = 4096
+M = 256
+N = 2048
+K = 16
+PIECE = 512
+TARGETS = N // K
+
+FLOPS = 2 * P * M * N
+
+
+def tile_lrgcn_batch_kernel(tc, table, w, ew, offs, out):
+    nc = tc.nc
+    with (
+        tc.tile_pool(name="held", bufs=1) as held,
+        tc.tile_pool(name="work", bufs=3) as work,
+        tc.psum_pool(name="psum", bufs=4) as psum,
+    ):
+        offsets = held.tile([P, N // 16], U16, name="offsets")
+        nc.sync.dma_start(offsets[:], offs)
+        table_sb = held.tile([P, NODES], BF16, name="table_sb")
+        nc.sync.dma_start(table_sb[:], table)
+        w_sb = held.tile([P, M], BF16, name="w_sb")
+        nc.scalar.dma_start(w_sb[:], w)
+        ew_all = held.tile([P, N], F32, name="ew_all")
+        nc.scalar.dma_start(ew_all[:], ew[0, :].partition_broadcast(P))
+
+        for block in range(M // P):
+            sums = work.tile([P, TARGETS], F32, name="sums")
+            for piece in range(N // PIECE):
+                y = psum.tile([P, PIECE], F32, name="y")
+                nc.tensor.matmul(
+                    y[:],
+                    w_sb[:, block * P : (block + 1) * P],
+                    table_sb[:].indirect(offsets[:, piece * PIECE // 16 : (piece + 1) * PIECE // 16]),
+                    start=True,
+                    stop=True,
+                )
+                weighted = work.tile([P, PIECE], F32, name="weighted")
+                nc.vector.tensor_tensor(
+                    weighted[:], y[:], ew_all[:, piece * PIECE : (piece + 1) * PIECE], ALU.mult
+                )
+                nc.vector.tensor_reduce(
+                    sums[:, piece * PIECE // K : (piece + 1) * PIECE // K],
+                    weighted[:].rearrange("p (n k) -> p n k", k=K),
+                    mybir.AxisListType.X,
+                    ALU.add,
+                )
+
+            negative = work.tile([P, TARGETS], F32, name="negative")
+            nc.vector.tensor_scalar_min(negative[:], sums[:], 0.0)
+            decayed = work.tile([P, TARGETS], F32, name="decayed")
+            nc.scalar.activation(decayed[:], negative[:], ACT.Exp, scale=1.0 / K)
+            positive = work.tile([P, TARGETS], F32, name="positive")
+            nc.vector.tensor_scalar(positive[:], sums[:], 0.0, 1.0 / K, ALU.max, ALU.mult)
+            result = work.tile([P, TARGETS], F32, name="result")
+            nc.vector.scalar_tensor_tensor(result[:], decayed[:], -1.0, positive[:], ALU.add, ALU.add)
+            nc.sync.dma_start(out[block * P : (block + 1) * P, :], result[:])

@@ -31,7 +31,11 @@ def tile_lrgcn_batch_kernel(tc, table, w, ew, offs, out):
         w_sb = held.tile([P, M], BF16, name="w_sb")
         nc.scalar.dma_start(w_sb[:], w)
         ew_all = held.tile([P, N], F32, name="ew_all")
-        nc.scalar.dma_start(ew_all[:], ew[0, :].partition_broadcast(P))
+        for piece in range(N // PIECE):
+            nc.sync.dma_start(
+                ew_all[:, piece * PIECE : (piece + 1) * PIECE],
+                ew[0, piece * PIECE : (piece + 1) * PIECE].partition_broadcast(P),
+            )
 
         for block in range(M // P):
             sums = work.tile([P, TARGETS], F32, name="sums")

@@ -19,9 +19,10 @@ FLOPS = 2 * P * M * N
 
 def tile_lrgcn_batch_kernel(tc, table, w, ew, offs, out):
     nc = tc.nc
+    pieces = N // PIECE
     with (
         tc.tile_pool(name="held", bufs=1) as held,
-        tc.tile_pool(name="work", bufs=3) as work,
+        tc.tile_pool(name="work", bufs=4) as work,
         tc.psum_pool(name="psum", bufs=4) as psum,
     ):
         offsets = held.tile([P, N // 16], U16, name="offsets")
@@ -31,40 +32,47 @@ def tile_lrgcn_batch_kernel(tc, table, w, ew, offs, out):
         w_sb = held.tile([P, M], BF16, name="w_sb")
         nc.scalar.dma_start(w_sb[:], w)
         ew_all = held.tile([P, N], F32, name="ew_all")
-        for piece in range(N // PIECE):
-            nc.sync.dma_start(
-                ew_all[:, piece * PIECE : (piece + 1) * PIECE],
-                ew[0, piece * PIECE : (piece + 1) * PIECE].partition_broadcast(P),
+        nc.scalar.dma_start(ew_all[:], ew[0, :].partition_broadcast(P))
+
+        z = [held.tile([P, TARGETS], F32, name=f"z{block}") for block in range(M // P)]
+
+        def sum_neighbours(block, piece, weighted):
+            nc.vector.tensor_reduce(
+                z[block][:, piece * PIECE // K : (piece + 1) * PIECE // K],
+                weighted[:].rearrange("p (n k) -> p n k", k=K),
+                mybir.AxisListType.X,
+                ALU.add,
             )
 
-        for block in range(M // P):
-            sums = work.tile([P, TARGETS], F32, name="sums")
-            for piece in range(N // PIECE):
-                y = psum.tile([P, PIECE], F32, name="y")
-                nc.tensor.matmul(
-                    y[:],
-                    w_sb[:, block * P : (block + 1) * P],
-                    table_sb[:].indirect(offsets[:, piece * PIECE // 16 : (piece + 1) * PIECE // 16]),
-                    start=True,
-                    stop=True,
-                )
-                weighted = work.tile([P, PIECE], F32, name="weighted")
-                nc.vector.tensor_tensor(
-                    weighted[:], y[:], ew_all[:, piece * PIECE : (piece + 1) * PIECE], ALU.mult
-                )
-                nc.vector.tensor_reduce(
-                    sums[:, piece * PIECE // K : (piece + 1) * PIECE // K],
-                    weighted[:].rearrange("p (n k) -> p n k", k=K),
-                    mybir.AxisListType.X,
-                    ALU.add,
-                )
-
+        def elu_and_store(block):
             negative = work.tile([P, TARGETS], F32, name="negative")
-            nc.vector.tensor_scalar_min(negative[:], sums[:], 0.0)
+            nc.vector.tensor_scalar_min(negative[:], z[block][:], 0.0)
             decayed = work.tile([P, TARGETS], F32, name="decayed")
-            nc.scalar.activation(decayed[:], negative[:], ACT.Exp, scale=1.0 / K)
-            positive = work.tile([P, TARGETS], F32, name="positive")
-            nc.vector.tensor_scalar(positive[:], sums[:], 0.0, 1.0 / K, ALU.max, ALU.mult)
+            nc.scalar.activation(decayed[:], negative[:], ACT.Exp)
             result = work.tile([P, TARGETS], F32, name="result")
-            nc.vector.scalar_tensor_tensor(result[:], decayed[:], -1.0, positive[:], ALU.add, ALU.add)
+            nc.vector.scalar_tensor_tensor(result[:], decayed[:], -1.0, z[block][:], ALU.add, ALU.max)
             nc.sync.dma_start(out[block * P : (block + 1) * P, :], result[:])
+
+        late = None
+        for piece in range(pieces):
+            looked_up = table_sb[:].indirect(offsets[:, piece * PIECE // 16 : (piece + 1) * PIECE // 16])
+            ew_piece = ew_all[:, piece * PIECE : (piece + 1) * PIECE]
+
+            y0 = psum.tile([P, PIECE], F32, name="y0")
+            nc.tensor.matmul(y0[:], w_sb[:, :P], looked_up, start=True, stop=True)
+            weighted0 = work.tile([P, PIECE], F32, name="weighted0")
+            nc.vector.scalar_tensor_tensor(weighted0[:], y0[:], 1.0 / K, ew_piece, ALU.mult, ALU.mult)
+            sum_neighbours(0, piece, weighted0)
+
+            y1 = psum.tile([P, PIECE], F32, name="y1")
+            nc.tensor.matmul(y1[:], w_sb[:, P:], looked_up, start=True, stop=True)
+            y1_sb = work.tile([P, PIECE], F32, name="y1_sb")
+            nc.scalar.activation(y1_sb[:], y1[:], ACT.Copy, scale=1.0 / K)
+            weighted1 = work.tile([P, PIECE], F32, name="weighted1")
+            nc.gpsimd.tensor_tensor(weighted1[:], y1_sb[:], ew_piece, ALU.mult)
+            if late is not None:
+                sum_neighbours(1, piece - 1, late)
+            late = weighted1
+        elu_and_store(0)
+        sum_neighbours(1, pieces - 1, late)
+        elu_and_store(1)

@@ -45,13 +45,17 @@ def tile_lrgcn_batch_kernel(tc, table, w, ew, offs, out):
             )
 
         def elu_and_store(block):
-            negative = work.tile([P, TARGETS], F32, name="negative")
-            nc.vector.tensor_scalar_min(negative[:], z[block][:], 0.0)
-            decayed = work.tile([P, TARGETS], F32, name="decayed")
-            nc.scalar.activation(decayed[:], negative[:], ACT.Exp)
-            result = work.tile([P, TARGETS], F32, name="result")
-            nc.vector.scalar_tensor_tensor(result[:], decayed[:], -1.0, z[block][:], ALU.add, ALU.max)
-            nc.sync.dma_start(out[block * P : (block + 1) * P, :], result[:])
+            grown = work.tile([P, TARGETS], F32, name="grown")
+            nc.scalar.activation(grown[:], z[block][:], ACT.Exp)
+            positive = work.tile([P, TARGETS], F32, name="positive")
+            nc.vector.tensor_scalar_max(positive[:], z[block][:], 0.0)
+
+            def finish():
+                result = work.tile([P, TARGETS], F32, name="result")
+                nc.vector.scalar_tensor_tensor(result[:], grown[:], -1.0, positive[:], ALU.add, ALU.min)
+                nc.sync.dma_start(out[block * P : (block + 1) * P, :], result[:])
+
+            return finish
 
         late = None
         for piece in range(pieces):
@@ -73,6 +77,7 @@ def tile_lrgcn_batch_kernel(tc, table, w, ew, offs, out):
             if late is not None:
                 sum_neighbours(1, piece - 1, late)
             late = weighted1
-        elu_and_store(0)
+        finish_block0 = elu_and_store(0)
         sum_neighbours(1, pieces - 1, late)
-        elu_and_store(1)
+        finish_block0()
+        elu_and_store(1)()

@@ -31,8 +31,9 @@ def tile_lrgcn_batch_kernel(tc, table, w, ew, offs, out):
         nc.sync.dma_start(table_sb[:], table)
         w_sb = held.tile([P, M], BF16, name="w_sb")
         nc.scalar.dma_start(w_sb[:], w)
-        ew_all = held.tile([P, N], F32, name="ew_all")
-        nc.scalar.dma_start(ew_all[:], ew[0, :].partition_broadcast(P))
+        ew_halves = [held.tile([P, N // 2], F32, name=f"ew_half{half}") for half in range(2)]
+        for half in range(2):
+            nc.scalar.dma_start(ew_halves[half][:], ew[0, half * N // 2 : (half + 1) * N // 2].partition_broadcast(P))
 
         z = [held.tile([P, TARGETS], F32, name=f"z{block}") for block in range(M // P)]
 
@@ -60,7 +61,8 @@ def tile_lrgcn_batch_kernel(tc, table, w, ew, offs, out):
         late = None
         for piece in range(pieces):
             looked_up = table_sb[:].indirect(offsets[:, piece * PIECE // 16 : (piece + 1) * PIECE // 16])
-            ew_piece = ew_all[:, piece * PIECE : (piece + 1) * PIECE]
+            in_half = piece % (pieces // 2)
+            ew_piece = ew_halves[piece // (pieces // 2)][:, in_half * PIECE : (in_half + 1) * PIECE]
 
             y0 = psum.tile([P, PIECE], F32, name="y0")
             nc.tensor.matmul(y0[:], w_sb[:, :P], looked_up, start=True, stop=True)

@@ -13,6 +13,7 @@ N = 2048
 K = 16
 PIECE = 512
 TARGETS = N // K
+WARM_UP = 7
 
 FLOPS = 2 * P * M * N
 
@@ -34,6 +35,12 @@ def tile_lrgcn_batch_kernel(tc, table, w, ew, offs, out):
         ew_halves = [held.tile([P, N // 2], F32, name=f"ew_half{half}") for half in range(2)]
         for half in range(2):
             nc.scalar.dma_start(ew_halves[half][:], ew[0, half * N // 2 : (half + 1) * N // 2].partition_broadcast(P))
+
+        zeros = held.tile([P, PIECE], BF16, name="zeros")
+        nc.vector.memset(zeros[:], 0.0)
+        unread = psum.tile([P, PIECE], F32, name="unread", tag="y0")
+        for _ in range(WARM_UP):
+            nc.tensor.matmul(unread[:], zeros[:, :P], zeros[:], start=True, stop=True)
 
         z = [held.tile([P, TARGETS], F32, name=f"z{block}") for block in range(M // P)]
 
@@ -58,7 +65,7 @@ def tile_lrgcn_batch_kernel(tc, table, w, ew, offs, out):
 
             return finish
 
-        late = None
+        waiting = []
         for piece in range(pieces):
             looked_up = table_sb[:].indirect(offsets[:, piece * PIECE // 16 : (piece + 1) * PIECE // 16])
             in_half = piece % (pieces // 2)
@@ -68,6 +75,8 @@ def tile_lrgcn_batch_kernel(tc, table, w, ew, offs, out):
             nc.tensor.matmul(y0[:], w_sb[:, :P], looked_up, start=True, stop=True)
             weighted0 = work.tile([P, PIECE], F32, name="weighted0")
             nc.vector.scalar_tensor_tensor(weighted0[:], y0[:], 1.0 / K, ew_piece, ALU.mult, ALU.mult)
+            if piece >= 2:
+                sum_neighbours(1, piece - 2, waiting[piece - 2])
             sum_neighbours(0, piece, weighted0)
 
             y1 = psum.tile([P, PIECE], F32, name="y1")
@@ -76,10 +85,9 @@ def tile_lrgcn_batch_kernel(tc, table, w, ew, offs, out):
             nc.scalar.activation(y1_sb[:], y1[:], ACT.Copy, scale=1.0 / K)
             weighted1 = work.tile([P, PIECE], F32, name="weighted1")
             nc.gpsimd.tensor_tensor(weighted1[:], y1_sb[:], ew_piece, ALU.mult)
-            if late is not None:
-                sum_neighbours(1, piece - 1, late)
-            late = weighted1
+            waiting.append(weighted1)
         finish_block0 = elu_and_store(0)
-        sum_neighbours(1, pieces - 1, late)
+        sum_neighbours(1, pieces - 2, waiting[pieces - 2])
+        sum_neighbours(1, pieces - 1, waiting[pieces - 1])
         finish_block0()
         elu_and_store(1)()

@@ -1,4 +1,5 @@
 import concourse.mybir as mybir
+from concourse.masks import make_identity
 
 BF16 = mybir.dt.bfloat16
 F32 = mybir.dt.float32
@@ -13,7 +14,10 @@ N = 2048
 K = 16
 PIECE = 512
 TARGETS = N // K
-WARM_UP = 7
+WARM_UP = 4
+ROWS = 16
+ROW = N // ROWS
+TERM_AT = (0, 32, 64)
 
 FLOPS = 2 * P * M * N
 
@@ -24,23 +28,63 @@ def tile_lrgcn_batch_kernel(tc, table, w, ew, offs, out):
     with (
         tc.tile_pool(name="held", bufs=1) as held,
         tc.tile_pool(name="work", bufs=4) as work,
-        tc.psum_pool(name="psum", bufs=4) as psum,
+        tc.psum_pool(name="psum", bufs=8) as psum,
     ):
         offsets = held.tile([P, N // 16], U16, name="offsets")
-        nc.sync.dma_start(offsets[:], offs)
         table_sb = held.tile([P, NODES], BF16, name="table_sb")
-        nc.sync.dma_start(table_sb[:], table)
         w_sb = held.tile([P, M], BF16, name="w_sb")
+        ew_rows = held.tile([P, ROW], F32, name="ew_rows")
+        for at in reversed(TERM_AT):
+            nc.sync.dma_start(ew_rows[at : at + ROWS, :], ew[0].rearrange("(r c) -> r c", c=ROW))
+        nc.sync.dma_start(offsets[:], offs)
+        nc.sync.dma_start(table_sb[:], table)
         nc.scalar.dma_start(w_sb[:], w)
-        ew_halves = [held.tile([P, N // 2], F32, name=f"ew_half{half}") for half in range(2)]
-        for half in range(2):
-            nc.scalar.dma_start(ew_halves[half][:], ew[0, half * N // 2 : (half + 1) * N // 2].partition_broadcast(P))
 
         zeros = held.tile([P, PIECE], BF16, name="zeros")
         nc.vector.memset(zeros[:], 0.0)
-        unread = psum.tile([P, PIECE], F32, name="unread", tag="y0")
+        unread = psum.tile([P, PIECE], F32, name="unread", tag="bank")
         for _ in range(WARM_UP):
             nc.tensor.matmul(unread[:], zeros[:, :P], zeros[:], start=True, stop=True)
+
+        first, second, third = [slice(at, at + ROWS) for at in TERM_AT]
+        terms = held.tile([P, ROW], BF16, name="terms")
+        nc.vector.memset(terms[:], 0.0)
+        lead = held.tile([P, ROW], BF16, name="lead")
+        left = held.tile([P, ROW], F32, name="left")
+        next_lead = held.tile([P, ROW], BF16, name="next_lead")
+        nc.vector.tensor_copy(lead[third, :], ew_rows[third, :])
+        nc.vector.tensor_tensor(left[third, :], ew_rows[third, :], lead[third, :], ALU.subtract)
+        nc.scalar.activation(lead[second, :], ew_rows[second, :], ACT.Copy)
+        nc.scalar.activation(terms[first, :], ew_rows[first, :], ACT.Copy)
+        nc.vector.tensor_copy(next_lead[third, :], left[third, :])
+        nc.vector.tensor_tensor(terms[second, :], ew_rows[second, :], lead[second, :], ALU.subtract)
+        nc.vector.tensor_tensor(terms[third, :], left[third, :], next_lead[third, :], ALU.subtract)
+
+        identity = held.tile([P, P], BF16, name="identity")
+        make_identity(nc, identity[:])
+        two_terms = held.tile([P, ROWS], BF16, name="two_terms")
+        chooser = held.tile([P, ROWS], BF16, name="chooser")
+        nc.gpsimd.tensor_tensor(two_terms[:], identity[:, first], identity[:, second], ALU.add)
+        nc.gpsimd.tensor_tensor(chooser[:], two_terms[:], identity[:, third], ALU.add)
+
+        ew_all = []
+        for piece in range(pieces):
+            handed_out = psum.tile([P, PIECE], F32, name="handed_out", tag="bank")
+            for part in range(PIECE // ROW):
+                row = piece * PIECE // ROW + part
+                nc.tensor.matmul(
+                    handed_out[:, part * ROW : (part + 1) * ROW],
+                    chooser[:, row : row + 1].to_broadcast([P, P]),
+                    terms[:],
+                    start=True,
+                    stop=True,
+                )
+            ew_piece = held.tile([P, PIECE], F32, name=f"ew_piece{piece}")
+            if piece % 2 == 0:
+                nc.vector.tensor_copy(ew_piece[:], handed_out[:])
+            else:
+                nc.scalar.activation(ew_piece[:], handed_out[:], ACT.Copy)
+            ew_all.append(ew_piece)
 
         z = [held.tile([P, TARGETS], F32, name=f"z{block}") for block in range(M // P)]
 
@@ -68,10 +112,9 @@ def tile_lrgcn_batch_kernel(tc, table, w, ew, offs, out):
         waiting = []
         for piece in range(pieces):
             looked_up = table_sb[:].indirect(offsets[:, piece * PIECE // 16 : (piece + 1) * PIECE // 16])
-            in_half = piece % (pieces // 2)
-            ew_piece = ew_halves[piece // (pieces // 2)][:, in_half * PIECE : (in_half + 1) * PIECE]
+            ew_piece = ew_all[piece][:]
 
-            y0 = psum.tile([P, PIECE], F32, name="y0")
+            y0 = psum.tile([P, PIECE], F32, name="y0", tag="bank")
             nc.tensor.matmul(y0[:], w_sb[:, :P], looked_up, start=True, stop=True)
             weighted0 = work.tile([P, PIECE], F32, name="weighted0")
             nc.vector.scalar_tensor_tensor(weighted0[:], y0[:], 1.0 / K, ew_piece, ALU.mult, ALU.mult)
@@ -79,7 +122,7 @@ def tile_lrgcn_batch_kernel(tc, table, w, ew, offs, out):
                 sum_neighbours(1, piece - 2, waiting[piece - 2])
             sum_neighbours(0, piece, weighted0)
 
-            y1 = psum.tile([P, PIECE], F32, name="y1")
+            y1 = psum.tile([P, PIECE], F32, name="y1", tag="bank")
             nc.tensor.matmul(y1[:], w_sb[:, P:], looked_up, start=True, stop=True)
             y1_sb = work.tile([P, PIECE], F32, name="y1_sb")
             nc.scalar.activation(y1_sb[:], y1[:], ACT.Copy, scale=1.0 / K)

@@ -36,8 +36,8 @@ def tile_lrgcn_batch_kernel(tc, table, w, ew, offs, out):
         ew_rows = held.tile([P, ROW], F32, name="ew_rows")
         for at in reversed(TERM_AT):
             nc.sync.dma_start(ew_rows[at : at + ROWS, :], ew[0].rearrange("(r c) -> r c", c=ROW))
-        nc.sync.dma_start(offsets[:], offs)
         nc.sync.dma_start(table_sb[:], table)
+        nc.sync.dma_start(offsets[:], offs)
         nc.scalar.dma_start(w_sb[:], w)
 
         zeros = held.tile([P, PIECE], BF16, name="zeros")
@@ -56,7 +56,7 @@ def tile_lrgcn_batch_kernel(tc, table, w, ew, offs, out):
         nc.vector.tensor_tensor(left[third, :], ew_rows[third, :], lead[third, :], ALU.subtract)
         nc.scalar.activation(lead[second, :], ew_rows[second, :], ACT.Copy)
         nc.scalar.activation(terms[first, :], ew_rows[first, :], ACT.Copy)
-        nc.vector.tensor_copy(next_lead[third, :], left[third, :])
+        nc.vector.tensor_tensor(next_lead[third, :], ew_rows[third, :], lead[third, :], ALU.subtract)
         nc.vector.tensor_tensor(terms[second, :], ew_rows[second, :], lead[second, :], ALU.subtract)
         nc.vector.tensor_tensor(terms[third, :], left[third, :], next_lead[third, :], ALU.subtract)
 
@@ -100,7 +100,10 @@ def tile_lrgcn_batch_kernel(tc, table, w, ew, offs, out):
             grown = work.tile([P, TARGETS], F32, name="grown")
             nc.scalar.activation(grown[:], z[block][:], ACT.Exp)
             positive = work.tile([P, TARGETS], F32, name="positive")
-            nc.vector.tensor_scalar_max(positive[:], z[block][:], 0.0)
+            if block == 0:
+                nc.scalar.activation(positive[:], z[block][:], ACT.Relu)
+            else:
+                nc.vector.tensor_scalar_max(positive[:], z[block][:], 0.0)
 
             def finish():
                 result = work.tile([P, TARGETS], F32, name="result")

@@ -12,7 +12,8 @@ NODES = 4096
 M = 256
 N = 2048
 K = 16
-PIECE = 512
+BANK = 512
+BANKS = N // BANK
 TARGETS = N // K
 WARM_UP = 4
 ROWS = 16
@@ -24,10 +25,9 @@ FLOPS = 2 * P * M * N
 
 def tile_lrgcn_batch_kernel(tc, table, w, ew, offs, out):
     nc = tc.nc
-    pieces = N // PIECE
     with (
         tc.tile_pool(name="held", bufs=1) as held,
-        tc.tile_pool(name="work", bufs=4) as work,
+        tc.tile_pool(name="work", bufs=1) as work,
         tc.psum_pool(name="psum", bufs=8) as psum,
     ):
         offsets = held.tile([P, N // 16], U16, name="offsets")
@@ -40,9 +40,9 @@ def tile_lrgcn_batch_kernel(tc, table, w, ew, offs, out):
         nc.sync.dma_start(offsets[:], offs)
         nc.scalar.dma_start(w_sb[:], w)
 
-        zeros = held.tile([P, PIECE], BF16, name="zeros")
+        zeros = held.tile([P, BANK], BF16, name="zeros")
         nc.vector.memset(zeros[:], 0.0)
-        unread = psum.tile([P, PIECE], F32, name="unread", tag="bank")
+        unread = psum.tile([P, BANK], F32, name="unread", tag="bank")
         for _ in range(WARM_UP):
             nc.tensor.matmul(unread[:], zeros[:, :P], zeros[:], start=True, stop=True)
 
@@ -67,11 +67,11 @@ def tile_lrgcn_batch_kernel(tc, table, w, ew, offs, out):
         nc.gpsimd.tensor_tensor(two_terms[:], identity[:, first], identity[:, second], ALU.add)
         nc.gpsimd.tensor_tensor(chooser[:], two_terms[:], identity[:, third], ALU.add)
 
-        ew_all = []
-        for piece in range(pieces):
-            handed_out = psum.tile([P, PIECE], F32, name="handed_out", tag="bank")
-            for part in range(PIECE // ROW):
-                row = piece * PIECE // ROW + part
+        ew_banks = []
+        for bank in range(BANKS):
+            handed_out = psum.tile([P, BANK], F32, name="handed_out", tag="bank")
+            for part in range(BANK // ROW):
+                row = bank * BANK // ROW + part
                 nc.tensor.matmul(
                     handed_out[:, part * ROW : (part + 1) * ROW],
                     chooser[:, row : row + 1].to_broadcast([P, P]),
@@ -79,61 +79,77 @@ def tile_lrgcn_batch_kernel(tc, table, w, ew, offs, out):
                     start=True,
                     stop=True,
                 )
-            ew_piece = held.tile([P, PIECE], F32, name=f"ew_piece{piece}")
-            if piece % 2 == 0:
-                nc.vector.tensor_copy(ew_piece[:], handed_out[:])
+            ew_bank = held.tile([P, BANK], F32, name=f"ew_bank{bank}")
+            if bank % 2 == 0:
+                nc.scalar.activation(ew_bank[:], handed_out[:], ACT.Copy)
             else:
-                nc.scalar.activation(ew_piece[:], handed_out[:], ACT.Copy)
-            ew_all.append(ew_piece)
+                nc.vector.tensor_copy(ew_bank[:], handed_out[:])
+            ew_banks.append(ew_bank)
 
         z = [held.tile([P, TARGETS], F32, name=f"z{block}") for block in range(M // P)]
 
-        def sum_neighbours(block, piece, weighted):
+        def sum_neighbours(block, bank):
             nc.vector.tensor_reduce(
-                z[block][:, piece * PIECE // K : (piece + 1) * PIECE // K],
-                weighted[:].rearrange("p (n k) -> p n k", k=K),
+                z[block][:, bank * BANK // K : (bank + 1) * BANK // K],
+                weighted[block][bank][:].rearrange("p (n k) -> p n k", k=K),
                 mybir.AxisListType.X,
                 ALU.add,
             )
 
         def elu_and_store(block):
-            grown = work.tile([P, TARGETS], F32, name="grown")
+            grown = work.tile([P, TARGETS], F32, name=f"grown{block}")
             nc.scalar.activation(grown[:], z[block][:], ACT.Exp)
-            positive = work.tile([P, TARGETS], F32, name="positive")
+            positive = work.tile([P, TARGETS], F32, name=f"positive{block}")
             if block == 0:
                 nc.scalar.activation(positive[:], z[block][:], ACT.Relu)
             else:
                 nc.vector.tensor_scalar_max(positive[:], z[block][:], 0.0)
 
             def finish():
-                result = work.tile([P, TARGETS], F32, name="result")
+                result = work.tile([P, TARGETS], F32, name=f"result{block}")
                 nc.vector.scalar_tensor_tensor(result[:], grown[:], -1.0, positive[:], ALU.add, ALU.min)
                 nc.sync.dma_start(out[block * P : (block + 1) * P, :], result[:])
 
             return finish
 
-        waiting = []
-        for piece in range(pieces):
-            looked_up = table_sb[:].indirect(offsets[:, piece * PIECE // 16 : (piece + 1) * PIECE // 16])
-            ew_piece = ew_all[piece][:]
+        weighted = [[work.tile([P, BANK], F32, name=f"weighted{block}_{bank}") for bank in range(BANKS)] for block in range(2)]
 
-            y0 = psum.tile([P, PIECE], F32, name="y0", tag="bank")
-            nc.tensor.matmul(y0[:], w_sb[:, :P], looked_up, start=True, stop=True)
-            weighted0 = work.tile([P, PIECE], F32, name="weighted0")
-            nc.vector.scalar_tensor_tensor(weighted0[:], y0[:], 1.0 / K, ew_piece, ALU.mult, ALU.mult)
-            if piece >= 2:
-                sum_neighbours(1, piece - 2, waiting[piece - 2])
-            sum_neighbours(0, piece, weighted0)
+        def look_up(block, bank, within):
+            columns = slice(bank * BANK + within.start, bank * BANK + within.stop)
+            y = psum.tile([P, BANK], F32, name="y", tag="bank")
+            nc.tensor.matmul(
+                y[:, within],
+                w_sb[:, block * P : (block + 1) * P],
+                table_sb[:].indirect(offsets[:, columns.start // 16 : columns.stop // 16]),
+                start=True,
+                stop=True,
+            )
+            return y[:, within]
 
-            y1 = psum.tile([P, PIECE], F32, name="y1", tag="bank")
-            nc.tensor.matmul(y1[:], w_sb[:, P:], looked_up, start=True, stop=True)
-            y1_sb = work.tile([P, PIECE], F32, name="y1_sb")
-            nc.scalar.activation(y1_sb[:], y1[:], ACT.Copy, scale=1.0 / K)
-            weighted1 = work.tile([P, PIECE], F32, name="weighted1")
-            nc.gpsimd.tensor_tensor(weighted1[:], y1_sb[:], ew_piece, ALU.mult)
-            waiting.append(weighted1)
+        def weigh_on_vector(bank, within):
+            y = look_up(0, bank, within)
+            nc.vector.scalar_tensor_tensor(
+                weighted[0][bank][:, within], y, 1.0 / K, ew_banks[bank][:, within], ALU.mult, ALU.mult
+            )
+
+        def weigh_on_gpsimd(bank, within):
+            y = look_up(1, bank, within)
+            y_sb = work.tile([P, BANK], F32, name=f"y_sb_{bank}_{within.start}")
+            nc.scalar.activation(y_sb[:, within], y, ACT.Copy, scale=1.0 / K)
+            nc.gpsimd.tensor_tensor(weighted[1][bank][:, within], y_sb[:, within], ew_banks[bank][:, within], ALU.mult)
+
+        for bank in range(BANKS):
+            weigh_on_vector(bank, slice(0, BANK))
+            if bank == 0:
+                weigh_on_gpsimd(bank, slice(0, BANK // 2))
+                weigh_on_gpsimd(bank, slice(BANK // 2, BANK))
+            else:
+                weigh_on_gpsimd(bank, slice(0, BANK))
+            if bank >= 2:
+                sum_neighbours(1, bank - 2)
+            sum_neighbours(0, bank)
         finish_block0 = elu_and_store(0)
-        sum_neighbours(1, pieces - 2, waiting[pieces - 2])
-        sum_neighbours(1, pieces - 1, waiting[pieces - 1])
+        sum_neighbours(1, BANKS - 2)
+        sum_neighbours(1, BANKS - 1)
         finish_block0()
         elu_and_store(1)()

@@ -36,9 +36,9 @@ def tile_lrgcn_batch_kernel(tc, table, w, ew, offs, out):
         ew_rows = held.tile([P, ROW], F32, name="ew_rows")
         for at in reversed(TERM_AT):
             nc.sync.dma_start(ew_rows[at : at + ROWS, :], ew[0].rearrange("(r c) -> r c", c=ROW))
+        nc.sync.dma_start(w_sb[:], w)
         nc.sync.dma_start(table_sb[:], table)
         nc.sync.dma_start(offsets[:], offs)
-        nc.scalar.dma_start(w_sb[:], w)
 
         zeros = held.tile([P, BANK], BF16, name="zeros")
         nc.vector.memset(zeros[:], 0.0)

@@ -63,9 +63,11 @@ def tile_lrgcn_batch_kernel(tc, table, w, ew, offs, out):
         identity = held.tile([P, P], BF16, name="identity")
         make_identity(nc, identity[:])
         two_terms = held.tile([P, ROWS], BF16, name="two_terms")
+        three_terms = held.tile([P, ROWS], BF16, name="three_terms")
         chooser = held.tile([P, ROWS], BF16, name="chooser")
         nc.gpsimd.tensor_tensor(two_terms[:], identity[:, first], identity[:, second], ALU.add)
-        nc.gpsimd.tensor_tensor(chooser[:], two_terms[:], identity[:, third], ALU.add)
+        nc.gpsimd.tensor_tensor(three_terms[:], two_terms[:], identity[:, third], ALU.add)
+        nc.gpsimd.tensor_scalar(chooser[:], three_terms[:], 1.0 / K, None, ALU.mult)
 
         ew_banks = []
         for bank in range(BANKS):
@@ -88,29 +90,34 @@ def tile_lrgcn_batch_kernel(tc, table, w, ew, offs, out):
 
         z = [held.tile([P, TARGETS], F32, name=f"z{block}") for block in range(M // P)]
 
-        def sum_neighbours(block, bank):
+        whole, halves = slice(0, BANK), (slice(0, BANK // 2), slice(BANK // 2, BANK))
+
+        def targets_of(bank, within):
+            return slice((bank * BANK + within.start) // K, (bank * BANK + within.stop) // K)
+
+        def sum_neighbours(block, bank, within):
             nc.vector.tensor_reduce(
-                z[block][:, bank * BANK // K : (bank + 1) * BANK // K],
-                weighted[block][bank][:].rearrange("p (n k) -> p n k", k=K),
+                z[block][:, targets_of(bank, within)],
+                weighted[block][bank][:, within].rearrange("p (n k) -> p n k", k=K),
                 mybir.AxisListType.X,
                 ALU.add,
             )
 
-        def elu_and_store(block):
-            grown = work.tile([P, TARGETS], F32, name=f"grown{block}")
-            nc.scalar.activation(grown[:], z[block][:], ACT.Exp)
-            positive = work.tile([P, TARGETS], F32, name=f"positive{block}")
-            if block == 0:
-                nc.scalar.activation(positive[:], z[block][:], ACT.Relu)
-            else:
-                nc.vector.tensor_scalar_max(positive[:], z[block][:], 0.0)
+        grown = [work.tile([P, TARGETS], F32, name=f"grown{block}") for block in range(2)]
+        positive = [work.tile([P, TARGETS], F32, name=f"positive{block}") for block in range(2)]
+        result = [work.tile([P, TARGETS], F32, name=f"result{block}") for block in range(2)]
 
-            def finish():
-                result = work.tile([P, TARGETS], F32, name=f"result{block}")
-                nc.vector.scalar_tensor_tensor(result[:], grown[:], -1.0, positive[:], ALU.add, ALU.min)
-                nc.sync.dma_start(out[block * P : (block + 1) * P, :], result[:])
+        def begin_elu(block, targets):
+            nc.scalar.activation(grown[block][:, targets], z[block][:, targets], ACT.Exp)
+            nc.scalar.activation(positive[block][:, targets], z[block][:, targets], ACT.Relu)
 
-            return finish
+        def end_elu(block, targets):
+            nc.vector.scalar_tensor_tensor(
+                result[block][:, targets], grown[block][:, targets], -1.0, positive[block][:, targets], ALU.add, ALU.min
+            )
+
+        def store(block):
+            nc.sync.dma_start(out[block * P : (block + 1) * P, :], result[block][:])
 
         weighted = [[work.tile([P, BANK], F32, name=f"weighted{block}_{bank}") for bank in range(BANKS)] for block in range(2)]
 
@@ -128,28 +135,34 @@ def tile_lrgcn_batch_kernel(tc, table, w, ew, offs, out):
 
         def weigh_on_vector(bank, within):
             y = look_up(0, bank, within)
-            nc.vector.scalar_tensor_tensor(
-                weighted[0][bank][:, within], y, 1.0 / K, ew_banks[bank][:, within], ALU.mult, ALU.mult
-            )
+            nc.vector.tensor_tensor(weighted[0][bank][:, within], y, ew_banks[bank][:, within], ALU.mult)
 
         def weigh_on_gpsimd(bank, within):
             y = look_up(1, bank, within)
             y_sb = work.tile([P, BANK], F32, name=f"y_sb_{bank}_{within.start}")
-            nc.scalar.activation(y_sb[:, within], y, ACT.Copy, scale=1.0 / K)
+            nc.scalar.activation(y_sb[:, within], y, ACT.Copy)
             nc.gpsimd.tensor_tensor(weighted[1][bank][:, within], y_sb[:, within], ew_banks[bank][:, within], ALU.mult)
 
+        final = BANKS - 1
         for bank in range(BANKS):
-            weigh_on_vector(bank, slice(0, BANK))
-            if bank == 0:
-                weigh_on_gpsimd(bank, slice(0, BANK // 2))
-                weigh_on_gpsimd(bank, slice(BANK // 2, BANK))
-            else:
-                weigh_on_gpsimd(bank, slice(0, BANK))
+            weigh_on_vector(bank, whole)
+            for within in halves if bank in (0, final) else (whole,):
+                weigh_on_gpsimd(bank, within)
             if bank >= 2:
-                sum_neighbours(1, bank - 2)
-            sum_neighbours(0, bank)
-        finish_block0 = elu_and_store(0)
-        sum_neighbours(1, BANKS - 2)
-        sum_neighbours(1, BANKS - 1)
-        finish_block0()
-        elu_and_store(1)()
+                sum_neighbours(1, bank - 2, whole)
+            sum_neighbours(0, bank, whole)
+        every = slice(0, TARGETS)
+        begin_elu(0, every)
+        sum_neighbours(1, final - 1, whole)
+        sum_neighbours(1, final, halves[0])
+        last = targets_of(final, halves[1])
+        earlier = slice(0, last.start)
+        begin_elu(1, earlier)
+        sum_neighbours(1, final, halves[1])
+        nc.scalar.activation(grown[1][:, last], z[1][:, last], ACT.Exp)
+        nc.vector.tensor_scalar_max(positive[1][:, last], z[1][:, last], 0.0)
+        end_elu(0, every)
+        store(0)
+        end_elu(1, earlier)
+        end_elu(1, last)
+        store(1)

@@ -15,6 +15,7 @@ K = 16
 BANK = 512
 BANKS = N // BANK
 TARGETS = N // K
+LEFT = 4
 WARM_UP = 4
 ROWS = 16
 ROW = N // ROWS
@@ -60,7 +61,7 @@ def tile_lrgcn_batch_kernel(tc, table, w, ew, offs, out):
         nc.vector.tensor_tensor(terms[second, :], ew_rows[second, :], lead[second, :], ALU.subtract)
         nc.vector.tensor_tensor(terms[third, :], left[third, :], next_lead[third, :], ALU.subtract)
 
-        identity = held.tile([P, P], BF16, name="identity")
+        identity = held.tile([P, P], F32, name="identity")
         make_identity(nc, identity[:])
         two_terms = held.tile([P, ROWS], BF16, name="two_terms")
         three_terms = held.tile([P, ROWS], BF16, name="three_terms")
@@ -133,9 +134,9 @@ def tile_lrgcn_batch_kernel(tc, table, w, ew, offs, out):
             )
             return y[:, within]
 
-        def weigh_on_vector(bank, within):
-            y = look_up(0, bank, within)
-            nc.vector.tensor_tensor(weighted[0][bank][:, within], y, ew_banks[bank][:, within], ALU.mult)
+        def weigh_on_vector(block, bank, within):
+            y = look_up(block, bank, within)
+            nc.vector.tensor_tensor(weighted[block][bank][:, within], y, ew_banks[bank][:, within], ALU.mult)
 
         def weigh_on_gpsimd(bank, within):
             y = look_up(1, bank, within)
@@ -145,16 +146,34 @@ def tile_lrgcn_batch_kernel(tc, table, w, ew, offs, out):
 
         final = BANKS - 1
         for bank in range(BANKS):
-            weigh_on_vector(bank, whole)
-            for within in halves if bank in (0, final) else (whole,):
-                weigh_on_gpsimd(bank, within)
-            if bank >= 2:
-                sum_neighbours(1, bank - 2, whole)
-            sum_neighbours(0, bank, whole)
+            if bank == 0:
+                weigh_on_vector(0, bank, whole)
+                weigh_on_vector(1, bank, halves[0])
+            else:
+                weigh_on_gpsimd(bank, halves[0])
+                weigh_on_vector(0, bank, whole)
+            weigh_on_gpsimd(bank, halves[1])
+            if bank >= 1:
+                sum_neighbours(0, bank - 1, whole)
+        sum_neighbours(0, final, whole)
+        def sum_on_tensor(bank):
+            left_over = psum.tile([P, BANK], F32, name="left_over", tag="bank")[:, : BANK // K * LEFT]
+            by_turn = weighted[1][bank][:].rearrange("p (n t r) -> p t n r", t=K // LEFT, r=LEFT)
+            for turn in range(K // LEFT):
+                nc.tensor.matmul(left_over, identity[:], by_turn[:, turn], start=turn == 0, stop=turn == K // LEFT - 1)
+            nc.vector.tensor_reduce(
+                z[1][:, targets_of(bank, whole)],
+                left_over.rearrange("p (n r) -> p n r", r=LEFT),
+                mybir.AxisListType.X,
+                ALU.add,
+            )
+
         every = slice(0, TARGETS)
         begin_elu(0, every)
-        sum_neighbours(1, final - 1, whole)
+        sum_neighbours(1, 2, whole)
+        sum_on_tensor(0)
         sum_neighbours(1, final, halves[0])
+        sum_on_tensor(1)
         last = targets_of(final, halves[1])
         earlier = slice(0, last.start)
         begin_elu(1, earlier)

import concourse.mybir as mybir
from concourse.masks import make_identity

BF16 = mybir.dt.bfloat16
F32 = mybir.dt.float32
U16 = mybir.dt.uint16
ALU = mybir.AluOpType
ACT = mybir.ActivationFunctionType

P = 128
NODES = 4096
M = 256
N = 2048
K = 16
BANK = 512
BANKS = N // BANK
TARGETS = N // K
LEFT = 4
WARM_UP = 4
ROWS = 16
ROW = N // ROWS
TERM_AT = (0, 32, 64)

FLOPS = 2 * P * M * N


def tile_lrgcn_batch_kernel(tc, table, w, ew, offs, out):
    nc = tc.nc
    with (
        tc.tile_pool(name="held", bufs=1) as held,
        tc.tile_pool(name="work", bufs=1) as work,
        tc.psum_pool(name="psum", bufs=8) as psum,
    ):
        offsets = held.tile([P, N // 16], U16, name="offsets")
        table_sb = held.tile([P, NODES], BF16, name="table_sb")
        w_sb = held.tile([P, M], BF16, name="w_sb")
        ew_rows = held.tile([P, ROW], F32, name="ew_rows")
        for at in reversed(TERM_AT):
            nc.sync.dma_start(ew_rows[at : at + ROWS, :], ew[0].rearrange("(r c) -> r c", c=ROW))
        nc.sync.dma_start(w_sb[:], w)
        nc.sync.dma_start(table_sb[:], table)
        nc.sync.dma_start(offsets[:], offs)

        zeros = held.tile([P, BANK], BF16, name="zeros")
        nc.vector.memset(zeros[:], 0.0)
        unread = psum.tile([P, BANK], F32, name="unread", tag="bank")
        for _ in range(WARM_UP):
            nc.tensor.matmul(unread[:], zeros[:, :P], zeros[:], start=True, stop=True)

        first, second, third = [slice(at, at + ROWS) for at in TERM_AT]
        terms = held.tile([P, ROW], BF16, name="terms")
        nc.vector.memset(terms[:], 0.0)
        lead = held.tile([P, ROW], BF16, name="lead")
        left = held.tile([P, ROW], F32, name="left")
        next_lead = held.tile([P, ROW], BF16, name="next_lead")
        nc.vector.tensor_copy(lead[third, :], ew_rows[third, :])
        nc.vector.tensor_tensor(left[third, :], ew_rows[third, :], lead[third, :], ALU.subtract)
        nc.scalar.activation(lead[second, :], ew_rows[second, :], ACT.Copy)
        nc.scalar.activation(terms[first, :], ew_rows[first, :], ACT.Copy)
        nc.vector.tensor_tensor(next_lead[third, :], ew_rows[third, :], lead[third, :], ALU.subtract)
        nc.vector.tensor_tensor(terms[second, :], ew_rows[second, :], lead[second, :], ALU.subtract)
        nc.vector.tensor_tensor(terms[third, :], left[third, :], next_lead[third, :], ALU.subtract)

        identity = held.tile([P, P], F32, name="identity")
        make_identity(nc, identity[:])
        two_terms = held.tile([P, ROWS], BF16, name="two_terms")
        three_terms = held.tile([P, ROWS], BF16, name="three_terms")
        chooser = held.tile([P, ROWS], BF16, name="chooser")
        nc.gpsimd.tensor_tensor(two_terms[:], identity[:, first], identity[:, second], ALU.add)
        nc.gpsimd.tensor_tensor(three_terms[:], two_terms[:], identity[:, third], ALU.add)
        nc.gpsimd.tensor_scalar(chooser[:], three_terms[:], 1.0 / K, None, ALU.mult)

        ew_banks = []
        for bank in range(BANKS):
            handed_out = psum.tile([P, BANK], F32, name="handed_out", tag="bank")
            for part in range(BANK // ROW):
                row = bank * BANK // ROW + part
                nc.tensor.matmul(
                    handed_out[:, part * ROW : (part + 1) * ROW],
                    chooser[:, row : row + 1].to_broadcast([P, P]),
                    terms[:],
                    start=True,
                    stop=True,
                )
            ew_bank = held.tile([P, BANK], F32, name=f"ew_bank{bank}")
            if bank % 2 == 0:
                nc.scalar.activation(ew_bank[:], handed_out[:], ACT.Copy)
            else:
                nc.vector.tensor_copy(ew_bank[:], handed_out[:])
            ew_banks.append(ew_bank)

        z = [held.tile([P, TARGETS], F32, name=f"z{block}") for block in range(M // P)]

        whole, halves = slice(0, BANK), (slice(0, BANK // 2), slice(BANK // 2, BANK))

        def targets_of(bank, within):
            return slice((bank * BANK + within.start) // K, (bank * BANK + within.stop) // K)

        def sum_neighbours(block, bank, within):
            nc.vector.tensor_reduce(
                z[block][:, targets_of(bank, within)],
                weighted[block][bank][:, within].rearrange("p (n k) -> p n k", k=K),
                mybir.AxisListType.X,
                ALU.add,
            )

        grown = [work.tile([P, TARGETS], F32, name=f"grown{block}") for block in range(2)]
        positive = [work.tile([P, TARGETS], F32, name=f"positive{block}") for block in range(2)]
        result = [work.tile([P, TARGETS], F32, name=f"result{block}") for block in range(2)]

        def begin_elu(block, targets):
            nc.scalar.activation(grown[block][:, targets], z[block][:, targets], ACT.Exp)
            nc.scalar.activation(positive[block][:, targets], z[block][:, targets], ACT.Relu)

        def end_elu(block, targets):
            nc.vector.scalar_tensor_tensor(
                result[block][:, targets], grown[block][:, targets], -1.0, positive[block][:, targets], ALU.add, ALU.min
            )

        def store(block):
            nc.sync.dma_start(out[block * P : (block + 1) * P, :], result[block][:])

        weighted = [[work.tile([P, BANK], F32, name=f"weighted{block}_{bank}") for bank in range(BANKS)] for block in range(2)]

        def look_up(block, bank, within):
            columns = slice(bank * BANK + within.start, bank * BANK + within.stop)
            y = psum.tile([P, BANK], F32, name="y", tag="bank")
            nc.tensor.matmul(
                y[:, within],
                w_sb[:, block * P : (block + 1) * P],
                table_sb[:].indirect(offsets[:, columns.start // 16 : columns.stop // 16]),
                start=True,
                stop=True,
            )
            return y[:, within]

        def weigh_on_vector(block, bank, within):
            y = look_up(block, bank, within)
            nc.vector.tensor_tensor(weighted[block][bank][:, within], y, ew_banks[bank][:, within], ALU.mult)

        def weigh_on_gpsimd(bank, within):
            y = look_up(1, bank, within)
            y_sb = work.tile([P, BANK], F32, name=f"y_sb_{bank}_{within.start}")
            nc.scalar.activation(y_sb[:, within], y, ACT.Copy)
            nc.gpsimd.tensor_tensor(weighted[1][bank][:, within], y_sb[:, within], ew_banks[bank][:, within], ALU.mult)

        final = BANKS - 1
        for bank in range(BANKS):
            if bank == 0:
                weigh_on_vector(0, bank, whole)
                weigh_on_vector(1, bank, halves[0])
            else:
                weigh_on_gpsimd(bank, halves[0])
                weigh_on_vector(0, bank, whole)
            weigh_on_gpsimd(bank, halves[1])
            if bank >= 1:
                sum_neighbours(0, bank - 1, whole)
        sum_neighbours(0, final, whole)
        def sum_on_tensor(bank):
            left_over = psum.tile([P, BANK], F32, name="left_over", tag="bank")[:, : BANK // K * LEFT]
            by_turn = weighted[1][bank][:].rearrange("p (n t r) -> p t n r", t=K // LEFT, r=LEFT)
            for turn in range(K // LEFT):
                nc.tensor.matmul(left_over, identity[:], by_turn[:, turn], start=turn == 0, stop=turn == K // LEFT - 1)
            nc.vector.tensor_reduce(
                z[1][:, targets_of(bank, whole)],
                left_over.rearrange("p (n r) -> p n r", r=LEFT),
                mybir.AxisListType.X,
                ALU.add,
            )

        every = slice(0, TARGETS)
        begin_elu(0, every)
        sum_neighbours(1, 2, whole)
        sum_on_tensor(0)
        sum_neighbours(1, final, halves[0])
        sum_on_tensor(1)
        last = targets_of(final, halves[1])
        earlier = slice(0, last.start)
        begin_elu(1, earlier)
        sum_neighbours(1, final, halves[1])
        nc.scalar.activation(grown[1][:, last], z[1][:, last], ACT.Exp)
        nc.vector.tensor_scalar_max(positive[1][:, last], z[1][:, last], 0.0)
        end_elu(0, every)
        store(0)
        end_elu(1, earlier)
        end_elu(1, last)
        store(1)
